import numpy as np
import ml_dtypes

BF16 = ml_dtypes.bfloat16


def bf(x):
    return np.asarray(x, np.float32).astype(BF16)


def f32(x):
    return np.asarray(x, np.float32)


def f64(x):
    return np.asarray(x).astype(np.float64)


def striped(idx):
    return np.tile(idx.reshape(-1, 16).T, (8, 1))


S, D, M, N, HQ, HKV = 512, 128, 256, 64, 4, 2
HALF = D // 2
NH = HQ + HKV
BASE = 10000.0


def spread():
    w = np.zeros((D, M))
    m = np.arange(D)
    w[m % HALF, m] = 1.0
    w[HALF + m % HALF, D + m] = np.where(m < HALF, -1.0, 1.0)
    return w


def setup_inputs():
    inv_freq = 1.0 / BASE ** (np.arange(HALF) / HALF)
    ang = np.outer(np.arange(S), inv_freq)
    return {"table": bf(np.concatenate([np.cos(ang), np.sin(ang)], axis=1)), "w": bf(spread()), "x": f32(np.random.standard_normal((NH * D, N))), "offs": striped(np.random.permutation(np.tile(np.arange(S), 2))[:N])}


def reference(table, w, x, offs):
    idx = offs[:16].T.reshape(-1)
    cs = f64(w).T @ f64(table)[idx].T
    c, s = cs[:D], cs[D:]
    xv = f64(x).reshape(NH, D, N)
    xr = np.concatenate([xv[:, HALF:], xv[:, :HALF]], axis=1)
    return (xv * c[None] + xr * s[None]).reshape(NH * D, N)

@@ -1,0 +1,80 @@
+import concourse.mybir as mybir
+from concourse.masks import make_identity
+
+P = 128
+S = 512
+N = 64
+NH = 6
+HALF = 64
+BLOCKS = S // P
+GH = NH // 2
+
+BF16, F32, U16 = mybir.dt.bfloat16, mybir.dt.float32, mybir.dt.uint16
+MULT, ADD = mybir.AluOpType.mult, mybir.AluOpType.add
+
+FLOPS = 2 * P * 2 * P * N
+
+
+def tile_openpangusinkattention_kernel(tc, table, w, x, offs, out):
+    nc = tc.nc
+    x_pairs = x.rearrange("(g h k i) j -> g i h k j", g=2, h=GH, k=2)
+    out_pairs = out.rearrange("(g h k i) j -> g k i h j", g=2, h=GH, k=2)
+    with (
+        tc.tile_pool(name="held", bufs=1) as held,
+        tc.psum_pool(name="psum", bufs=1) as psum,
+    ):
+        rows = [held.tile([P, P], BF16, name=f"rows{b}") for b in range(BLOCKS)]
+        for b in range(BLOCKS):
+            queue = nc.sync if b < BLOCKS // 2 else nc.scalar
+            queue.dma_start(rows[b][:], table[b * P : (b + 1) * P, :])
+
+        offsets = held.tile([P, N // 16], U16, name="offsets")
+        nc.sync.dma_start(offsets[:], offs)
+        weights = held.tile([P, 2 * P], BF16, name="weights")
+        nc.scalar.dma_start(weights[:], w)
+
+        x_both = held.tile([P, GH, 2, N], F32, name="x_both")
+        nc.sync.dma_start(x_both[0:HALF], x_pairs[0])
+        nc.scalar.dma_start(x_both[HALF:P], x_pairs[1])
+
+        identity = held.tile([P, P], BF16, name="identity")
+        make_identity(nc, identity[:])
+
+        sign = held.tile([P, 2], F32, name="sign")
+        nc.vector.memset(sign[0:HALF, 0:1], 1.0)
+        nc.vector.memset(sign[HALF:P, 0:1], -1.0)
+        nc.vector.memset(sign[0:HALF, 1:2], -1.0)
+        nc.vector.memset(sign[HALF:P, 1:2], 1.0)
+
+        window = held.tile([P, S], BF16, name="window")
+        for half in range(2):
+            flipped = psum.tile([P, 2 * P], BF16, name=f"flipped{half}")
+            for b in range(2):
+                nc.tensor.transpose(flipped[:, b * P : (b + 1) * P], rows[2 * half + b][:], identity[:])
+            nc.vector.tensor_copy(window[:, half * 2 * P : (half + 1) * 2 * P], flipped[:])
+
+        cs = [psum.tile([P, N], F32, name=f"cs{c}") for c in range(2)]
+        for c in range(2):
+            nc.tensor.matmul(
+                cs[c][:],
+                weights[:, c * P : (c + 1) * P],
+                window[:].indirect(offsets[:]),
+                start=True,
+                stop=True,
+            )
+
+        by_cos = held.tile([P, GH, 2, N], F32, name="by_cos")
+        cos = cs[0][:].unsqueeze(1).unsqueeze(1).to_broadcast([P, GH, 2, N])
+        nc.vector.tensor_tensor(by_cos[:], x_both[:], cos, MULT)
+        sin = cs[1][:].unsqueeze(1).to_broadcast([P, GH, N])
+        by_sin = [held.tile([P, GH, N], F32, name=f"by_sin{k}") for k in range(2)]
+        for k in range(2):
+            nc.vector.tensor_tensor(by_sin[k][:], x_both[:, :, 1 - k, :], sin, MULT)
+
+        for k in range(2):
+            rotated = held.tile([P, GH, N], F32, name=f"rotated{k}")
+            nc.vector.scalar_tensor_tensor(
+                rotated[:], by_sin[k][:], sign[:, k : k + 1], by_cos[:, :, k, :], op0=MULT, op1=ADD
+            )
+            nc.sync.dma_start(out_pairs[0, k], rotated[0:HALF])
+            nc.scalar.dma_start(out_pairs[1, k], rotated[HALF:P])

@@ -10,15 +10,15 @@ BLOCKS = S // P
 GH = NH // 2
 
 BF16, F32, U16 = mybir.dt.bfloat16, mybir.dt.float32, mybir.dt.uint16
-MULT, ADD = mybir.AluOpType.mult, mybir.AluOpType.add
+MULT, ADD, SUBTRACT = mybir.AluOpType.mult, mybir.AluOpType.add, mybir.AluOpType.subtract
 
 FLOPS = 2 * P * 2 * P * N
 
 
 def tile_openpangusinkattention_kernel(tc, table, w, x, offs, out):
     nc = tc.nc
-    x_pairs = x.rearrange("(g h k i) j -> g i h k j", g=2, h=GH, k=2)
-    out_pairs = out.rearrange("(g h k i) j -> g k i h j", g=2, h=GH, k=2)
+    x_rows = x.rearrange("(g h k i) j -> g k i h j", g=2, h=GH, k=2)
+    out_rows = out.rearrange("(g h k i) j -> g k i h j", g=2, h=GH, k=2)
     with (
         tc.tile_pool(name="held", bufs=1) as held,
         tc.psum_pool(name="psum", bufs=1) as psum,
@@ -33,18 +33,14 @@ def tile_openpangusinkattention_kernel(tc, table, w, x, offs, out):
         weights = held.tile([P, 2 * P], BF16, name="weights")
         nc.scalar.dma_start(weights[:], w)
 
-        x_both = held.tile([P, GH, 2, N], F32, name="x_both")
-        nc.sync.dma_start(x_both[0:HALF], x_pairs[0])
-        nc.scalar.dma_start(x_both[HALF:P], x_pairs[1])
-
         identity = held.tile([P, P], BF16, name="identity")
         make_identity(nc, identity[:])
 
-        sign = held.tile([P, 2], F32, name="sign")
-        nc.vector.memset(sign[0:HALF, 0:1], 1.0)
-        nc.vector.memset(sign[HALF:P, 0:1], -1.0)
-        nc.vector.memset(sign[0:HALF, 1:2], -1.0)
-        nc.vector.memset(sign[HALF:P, 1:2], 1.0)
+        x_slot = [held.tile([P, GH, N], F32, name=f"x_slot{t}") for t in range(2)]
+        nc.sync.dma_start(x_slot[0][0:HALF], x_rows[0, 0])
+        nc.scalar.dma_start(x_slot[0][HALF:P], x_rows[1, 1])
+        nc.gpsimd.dma_start(x_slot[1][0:HALF], x_rows[0, 1])
+        nc.gpsimd.dma_start(x_slot[1][HALF:P], x_rows[1, 0])
 
         window = held.tile([P, S], BF16, name="window")
         for half in range(2):
@@ -63,18 +59,15 @@ def tile_openpangusinkattention_kernel(tc, table, w, x, offs, out):
                 stop=True,
             )
 
-        by_cos = held.tile([P, GH, 2, N], F32, name="by_cos")
-        cos = cs[0][:].unsqueeze(1).unsqueeze(1).to_broadcast([P, GH, 2, N])
-        nc.vector.tensor_tensor(by_cos[:], x_both[:], cos, MULT)
-        sin = cs[1][:].unsqueeze(1).to_broadcast([P, GH, N])
-        by_sin = [held.tile([P, GH, N], F32, name=f"by_sin{k}") for k in range(2)]
-        for k in range(2):
-            nc.vector.tensor_tensor(by_sin[k][:], x_both[:, :, 1 - k, :], sin, MULT)
+        cos, sin = [cs[c][:].unsqueeze(1).to_broadcast([P, GH, N]) for c in range(2)]
+        by_cos = [held.tile([P, GH, N], F32, name=f"by_cos{t}") for t in range(2)]
+        by_sin = [held.tile([P, GH, N], F32, name=f"by_sin{t}") for t in range(2)]
+        for t in range(2):
+            nc.vector.tensor_tensor(by_cos[t][:], x_slot[t][:], cos, MULT)
+            nc.vector.tensor_tensor(by_sin[t][:], x_slot[t][:], sin, MULT)
 
-        for k in range(2):
-            rotated = held.tile([P, GH, N], F32, name=f"rotated{k}")
-            nc.vector.scalar_tensor_tensor(
-                rotated[:], by_sin[k][:], sign[:, k : k + 1], by_cos[:, :, k, :], op0=MULT, op1=ADD
-            )
-            nc.sync.dma_start(out_pairs[0, k], rotated[0:HALF])
-            nc.scalar.dma_start(out_pairs[1, k], rotated[HALF:P])
+        for t, op in enumerate((ADD, SUBTRACT)):
+            rotated = held.tile([P, GH, N], F32, name=f"rotated{t}")
+            nc.vector.tensor_tensor(rotated[:], by_cos[t][:], by_sin[1 - t][:], op)
+            nc.sync.dma_start(out_rows[0, t], rotated[0:HALF])
+            nc.scalar.dma_start(out_rows[1, 1 - t], rotated[HALF:P])

@@ -6,7 +6,6 @@ S = 512
 N = 64
 NH = 6
 HALF = 64
-BLOCKS = S // P
 GH = NH // 2
 
 BF16, F32, U16 = mybir.dt.bfloat16, mybir.dt.float32, mybir.dt.uint16
@@ -23,10 +22,10 @@ def tile_openpangusinkattention_kernel(tc, table, w, x, offs, out):
         tc.tile_pool(name="held", bufs=1) as held,
         tc.psum_pool(name="psum", bufs=1) as psum,
     ):
-        rows = [held.tile([P, P], BF16, name=f"rows{b}") for b in range(BLOCKS)]
-        for b in range(BLOCKS):
-            queue = nc.sync if b < BLOCKS // 2 else nc.scalar
-            queue.dma_start(rows[b][:], table[b * P : (b + 1) * P, :])
+        rows = [held.tile([P, 2, P], BF16, name=f"rows{half}") for half in range(2)]
+        table_halves = table.rearrange("(half b p) d -> half p b d", half=2, b=2)
+        for half, queue in enumerate((nc.sync, nc.scalar)):
+            queue.dma_start(rows[half][:], table_halves[half])
 
         offsets = held.tile([P, N // 16], U16, name="offsets")
         nc.sync.dma_start(offsets[:], offs)
@@ -37,16 +36,15 @@ def tile_openpangusinkattention_kernel(tc, table, w, x, offs, out):
         make_identity(nc, identity[:])
 
         x_slot = [held.tile([P, GH, N], F32, name=f"x_slot{t}") for t in range(2)]
-        nc.sync.dma_start(x_slot[0][0:HALF], x_rows[0, 0])
-        nc.scalar.dma_start(x_slot[0][HALF:P], x_rows[1, 1])
-        nc.gpsimd.dma_start(x_slot[1][0:HALF], x_rows[0, 1])
-        nc.gpsimd.dma_start(x_slot[1][HALF:P], x_rows[1, 0])
+        for t in range(2):
+            nc.sync.dma_start(x_slot[t][0:HALF], x_rows[0, t])
+            nc.scalar.dma_start(x_slot[t][HALF:P], x_rows[1, 1 - t])
 
         window = held.tile([P, S], BF16, name="window")
         for half in range(2):
             flipped = psum.tile([P, 2 * P], BF16, name=f"flipped{half}")
             for b in range(2):
-                nc.tensor.transpose(flipped[:, b * P : (b + 1) * P], rows[2 * half + b][:], identity[:])
+                nc.tensor.transpose(flipped[:, b * P : (b + 1) * P], rows[half][:, b, :], identity[:])
             nc.vector.tensor_copy(window[:, half * 2 * P : (half + 1) * 2 * P], flipped[:])
 
         cs = [psum.tile([P, N], F32, name=f"cs{c}") for c in range(2)]

@@ -60,12 +60,15 @@ def tile_openpangusinkattention_kernel(tc, table, w, x, offs, out):
         cos, sin = [cs[c][:].unsqueeze(1).to_broadcast([P, GH, N]) for c in range(2)]
         by_cos = [held.tile([P, GH, N], F32, name=f"by_cos{t}") for t in range(2)]
         by_sin = [held.tile([P, GH, N], F32, name=f"by_sin{t}") for t in range(2)]
-        for t in range(2):
-            nc.vector.tensor_tensor(by_cos[t][:], x_slot[t][:], cos, MULT)
-            nc.vector.tensor_tensor(by_sin[t][:], x_slot[t][:], sin, MULT)
+        rotated = [held.tile([P, GH, N], F32, name=f"rotated{t}") for t in range(2)]
 
-        for t, op in enumerate((ADD, SUBTRACT)):
-            rotated = held.tile([P, GH, N], F32, name=f"rotated{t}")
-            nc.vector.tensor_tensor(rotated[:], by_cos[t][:], by_sin[1 - t][:], op)
-            nc.sync.dma_start(out_rows[0, t], rotated[0:HALF])
-            nc.scalar.dma_start(out_rows[1, 1 - t], rotated[HALF:P])
+        nc.vector.tensor_tensor(by_cos[0][:], x_slot[0][:], cos, MULT)
+        nc.vector.tensor_tensor(by_sin[1][:], x_slot[1][:], sin, MULT)
+        nc.vector.tensor_tensor(by_sin[0][:], x_slot[0][:], sin, MULT)
+        nc.vector.tensor_tensor(rotated[0][:], by_cos[0][:], by_sin[1][:], ADD)
+        nc.sync.dma_start(out_rows[0, 0], rotated[0][0:HALF])
+        nc.scalar.dma_start(out_rows[1, 1], rotated[0][HALF:P])
+        nc.vector.tensor_tensor(by_cos[1][:], x_slot[1][:], cos, MULT)
+        nc.vector.tensor_tensor(rotated[1][:], by_cos[1][:], by_sin[0][:], SUBTRACT)
+        nc.sync.dma_start(out_rows[0, 1], rotated[1][0:HALF])
+        nc.scalar.dma_start(out_rows[1, 0], rotated[1][HALF:P])

@@ -67,8 +67,8 @@ def tile_openpangusinkattention_kernel(tc, table, w, x, offs, out):
         nc.vector.tensor_tensor(by_sin[0][:], x_slot[0][:], sin, MULT)
         nc.vector.tensor_tensor(rotated[0][:], by_cos[0][:], by_sin[1][:], ADD)
         nc.sync.dma_start(out_rows[0, 0], rotated[0][0:HALF])
-        nc.scalar.dma_start(out_rows[1, 1], rotated[0][HALF:P])
+        nc.sync.dma_start(out_rows[1, 1], rotated[0][HALF:P])
         nc.vector.tensor_tensor(by_cos[1][:], x_slot[1][:], cos, MULT)
         nc.vector.tensor_tensor(rotated[1][:], by_cos[1][:], by_sin[0][:], SUBTRACT)
-        nc.sync.dma_start(out_rows[0, 1], rotated[1][0:HALF])
+        nc.scalar.dma_start(out_rows[0, 1], rotated[1][0:HALF])
         nc.scalar.dma_start(out_rows[1, 0], rotated[1][HALF:P])

@@ -38,7 +38,7 @@ def tile_openpangusinkattention_kernel(tc, table, w, x, offs, out):
         x_slot = [held.tile([P, GH, N], F32, name=f"x_slot{t}") for t in range(2)]
         for t in range(2):
             nc.sync.dma_start(x_slot[t][0:HALF], x_rows[0, t])
-            nc.scalar.dma_start(x_slot[t][HALF:P], x_rows[1, 1 - t])
+            nc.sync.dma_start(x_slot[t][HALF:P], x_rows[1, 1 - t])
 
         window = held.tile([P, S], BF16, name="window")
         for half in range(2):

import concourse.mybir as mybir
from concourse.masks import make_identity

P = 128
S = 512
N = 64
NH = 6
HALF = 64
GH = NH // 2

BF16, F32, U16 = mybir.dt.bfloat16, mybir.dt.float32, mybir.dt.uint16
MULT, ADD, SUBTRACT = mybir.AluOpType.mult, mybir.AluOpType.add, mybir.AluOpType.subtract

FLOPS = 2 * P * 2 * P * N


def tile_openpangusinkattention_kernel(tc, table, w, x, offs, out):
    nc = tc.nc
    x_rows = x.rearrange("(g h k i) j -> g k i h j", g=2, h=GH, k=2)
    out_rows = out.rearrange("(g h k i) j -> g k i h j", g=2, h=GH, k=2)
    with (
        tc.tile_pool(name="held", bufs=1) as held,
        tc.psum_pool(name="psum", bufs=1) as psum,
    ):
        rows = [held.tile([P, 2, P], BF16, name=f"rows{half}") for half in range(2)]
        table_halves = table.rearrange("(half b p) d -> half p b d", half=2, b=2)
        for half, queue in enumerate((nc.sync, nc.scalar)):
            queue.dma_start(rows[half][:], table_halves[half])

        offsets = held.tile([P, N // 16], U16, name="offsets")
        nc.sync.dma_start(offsets[:], offs)
        weights = held.tile([P, 2 * P], BF16, name="weights")
        nc.scalar.dma_start(weights[:], w)

        identity = held.tile([P, P], BF16, name="identity")
        make_identity(nc, identity[:])

        x_slot = [held.tile([P, GH, N], F32, name=f"x_slot{t}") for t in range(2)]
        for t in range(2):
            nc.sync.dma_start(x_slot[t][0:HALF], x_rows[0, t])
            nc.sync.dma_start(x_slot[t][HALF:P], x_rows[1, 1 - t])

        window = held.tile([P, S], BF16, name="window")
        for half in range(2):
            flipped = psum.tile([P, 2 * P], BF16, name=f"flipped{half}")
            for b in range(2):
                nc.tensor.transpose(flipped[:, b * P : (b + 1) * P], rows[half][:, b, :], identity[:])
            nc.vector.tensor_copy(window[:, half * 2 * P : (half + 1) * 2 * P], flipped[:])

        cs = [psum.tile([P, N], F32, name=f"cs{c}") for c in range(2)]
        for c in range(2):
            nc.tensor.matmul(
                cs[c][:],
                weights[:, c * P : (c + 1) * P],
                window[:].indirect(offsets[:]),
                start=True,
                stop=True,
            )

        cos, sin = [cs[c][:].unsqueeze(1).to_broadcast([P, GH, N]) for c in range(2)]
        by_cos = [held.tile([P, GH, N], F32, name=f"by_cos{t}") for t in range(2)]
        by_sin = [held.tile([P, GH, N], F32, name=f"by_sin{t}") for t in range(2)]
        rotated = [held.tile([P, GH, N], F32, name=f"rotated{t}") for t in range(2)]

        nc.vector.tensor_tensor(by_cos[0][:], x_slot[0][:], cos, MULT)
        nc.vector.tensor_tensor(by_sin[1][:], x_slot[1][:], sin, MULT)
        nc.vector.tensor_tensor(by_sin[0][:], x_slot[0][:], sin, MULT)
        nc.vector.tensor_tensor(rotated[0][:], by_cos[0][:], by_sin[1][:], ADD)
        nc.sync.dma_start(out_rows[0, 0], rotated[0][0:HALF])
        nc.sync.dma_start(out_rows[1, 1], rotated[0][HALF:P])
        nc.vector.tensor_tensor(by_cos[1][:], x_slot[1][:], cos, MULT)
        nc.vector.tensor_tensor(rotated[1][:], by_cos[1][:], by_sin[0][:], SUBTRACT)
        nc.scalar.dma_start(out_rows[0, 1], rotated[1][0:HALF])
        nc.scalar.dma_start(out_rows[1, 0], rotated[1][HALF:P])
